import numpy as np
import ml_dtypes


def mxq(x, axis, fmt="e4m3"):
    dtype, down = {"e4m3": (ml_dtypes.float8_e4m3fn, 7), "e5m2": (ml_dtypes.float8_e5m2, 14)}[fmt]
    v = np.moveaxis(np.asarray(x, np.float32).astype(ml_dtypes.bfloat16).astype(np.float64), axis, -1)
    blocks = v.reshape(v.shape[:-1] + (-1, 32))
    amax = np.abs(blocks).max(-1, keepdims=True)
    byte = np.maximum(np.where(amax > 0, np.frexp(amax)[1] - 1 + 127, 0) - down, 1)
    scale = np.exp2(byte - 127.0)
    codes = (blocks / scale).astype(np.float32).astype(dtype).astype(np.float64)
    return np.moveaxis((codes * scale).reshape(v.shape), -1, axis)


WIDE = False


def mx_kscale(k):
    if not WIDE:
        return np.ones(k)
    levels = np.array([10, -10, 5, -5, 0])
    a = np.random.permutation(np.resize(levels, k // 512 * 4)).reshape(k // 512, 4)
    idx = np.arange(k)
    return np.exp2(a[idx // 512, idx % 128 // 32])


BF16 = ml_dtypes.bfloat16


def bf(x):
    return np.asarray(x, np.float32).astype(BF16)


def f64(x):
    return np.asarray(x).astype(np.float64)


E2M1 = np.array([0.0, 0.5, 1.0, 1.5, 2.0, 3.0, 4.0, 6.0, -0.0, -0.5, -1.0, -1.5, -2.0, -3.0, -4.0, -6.0])


def pack_weight(w, fmt):
    k, n = w.shape
    w = f64(bf(w)).reshape(k // 32, 32, n)
    amax = np.abs(w).max(1)
    if fmt == "e4m3":
        byte = np.frexp(amax)[1] - 1 + 127 - 7
    else:
        mant, ex = np.frexp(amax / 6.0)
        byte = np.where(mant > 0.5, ex, ex - 1) + 127
    byte = np.clip(np.where(amax > 0, byte, 1), 1, 254)
    scaled = (w * np.exp2(127.0 - byte)[:, None, :]).reshape(k, n).astype(np.float32)
    by_word = np.ascontiguousarray(scaled.reshape(k // 512, 128, 4, n).transpose(0, 1, 3, 2))
    if fmt == "e4m3":
        words = by_word.astype(ml_dtypes.float8_e4m3fn).view(np.uint8)
    else:
        c = by_word.astype(ml_dtypes.float4_e2m1fn).view(np.uint8) & 0xF
        words = c[..., 0::2] | (c[..., 1::2] << 4)
    return np.ascontiguousarray(words), np.ascontiguousarray(byte.astype(np.uint8).reshape(k // 512, 16, n))


def unpack_weight(words, scales, fmt):
    g, p, n, _ = words.shape
    if fmt == "e4m3":
        vals = np.ascontiguousarray(words).view(ml_dtypes.float8_e4m3fn).astype(np.float64)
    else:
        nib = np.empty((g, p, n, 4), np.uint8)
        nib[..., 0::2] = words & 0xF
        nib[..., 1::2] = words >> 4
        vals = E2M1[nib]
    vals = vals * np.repeat(np.exp2(scales.astype(np.float64) - 127.0), 8, axis=1)[..., None]
    return vals.transpose(0, 1, 3, 2).reshape(g * 512, n)


B, D, H = 128, 8192, 512
PASS = 512
MX_REC = H % PASS == 0


def sigmoid(v):
    return 1.0 / (1.0 + np.exp(-v))


def setup_inputs():
    s = mx_kscale(D)
    r = mx_kscale(H) if MX_REC else np.ones(H)
    gate_b = np.concatenate([np.zeros(H), np.zeros(H), np.ones(H), np.zeros(H)])
    x_t = bf(np.random.standard_normal((B, D)) * s)
    h_prev = bf(np.random.standard_normal((B, H)) * r)
    c_prev = bf(np.random.standard_normal((B, H)))
    n_prev = bf(0.5 + np.abs(np.random.standard_normal((B, H))))
    W_words, W_scales = pack_weight(np.random.standard_normal((D, 4 * H)) / np.sqrt(D) / s[:, None], "e4m3")
    R_words, R_scales = pack_weight(np.random.standard_normal((H, 4 * H)) / np.sqrt(H) / r[:, None], "e4m3")
    b = bf(gate_b + 0.2 * np.random.standard_normal(4 * H))
    return {"x_t": x_t,
            "h_prev": h_prev,
            "c_prev": c_prev,
            "n_prev": n_prev,
            "W_words": W_words,
            "W_scales": W_scales,
            "R_words": R_words,
            "R_scales": R_scales,
            "b": b}


def reference(x_t, h_prev, c_prev, n_prev, W_words, W_scales, R_words, R_scales, b):
    inp = mxq(f64(x_t), 1, "e4m3") @ unpack_weight(W_words, W_scales, "e4m3")
    if MX_REC:
        rec = mxq(f64(h_prev), 1, "e4m3") @ unpack_weight(R_words, R_scales, "e4m3")
    else:
        rec = f64(h_prev) @ unpack_weight(R_words, R_scales, "e4m3")
    pre = inp + rec + f64(b)
    z_tilde, i_tilde, f_tilde, o_tilde = np.split(pre, 4, axis=-1)
    z_t = np.tanh(z_tilde)
    i_t = np.minimum(np.exp(i_tilde), 50.0)
    f_t = sigmoid(f_tilde)
    o_t = sigmoid(o_tilde)
    c_t = f_t * f64(c_prev) + i_t * z_t
    n_t = f_t * f64(n_prev) + i_t
    h_t = o_t * (c_t / (n_t + 1e-6))
    return h_t, c_t, n_t

@@ -1,0 +1,215 @@
+from contextlib import ExitStack
+
+import concourse.mybir as mybir
+from concourse.masks import make_identity
+
+F32 = mybir.dt.float32
+BF16 = mybir.dt.bfloat16
+I32 = mybir.dt.int32
+U32 = mybir.dt.uint32
+U8 = mybir.dt.uint8
+FP8X4 = mybir.dt.float8_e4m3fn_x4
+ACT = mybir.ActivationFunctionType
+ALU = mybir.AluOpType
+
+P = 128
+PACK = 4
+K_PASS = P * PACK
+D = 8192
+H = 512
+X_GROUPS = D // K_PASS
+GROUPS = X_GROUPS + 1
+Z, I, F, O = 0, 1, 2, 3
+GATES = 4
+WORDS_PER_GROUP = K_PASS // 2
+CHUNK = 4
+PLANES_PER_SLOT = 4
+SLOTS = (GROUPS + PLANES_PER_SLOT - 1) // PLANES_PER_SLOT
+
+FLOPS = 2 * P * (D + H) * GATES * H
+
+
+def gate_columns(gate):
+    return slice(gate * H, (gate + 1) * H)
+
+
+def tile_slstmcell_k_kernel(
+    tc, x_t, h_prev, c_prev, n_prev, W_words, W_scales, R_words, R_scales, b, out_0, out_1, out_2
+):
+    nc = tc.nc
+    with ExitStack() as ctx:
+        consts = ctx.enter_context(tc.tile_pool(name="consts", bufs=1))
+        weights = ctx.enter_context(tc.tile_pool(name="weights", bufs=1))
+        acts = ctx.enter_context(tc.tile_pool(name="acts", bufs=1))
+        stage = ctx.enter_context(tc.tile_pool(name="stage", bufs=2))
+        cell = ctx.enter_context(tc.tile_pool(name="cell", bufs=1))
+        gate_psum = ctx.enter_context(tc.psum_pool(name="gate_psum", bufs=1))
+        work_psum = ctx.enter_context(tc.psum_pool(name="work_psum", bufs=4))
+
+        warm = consts.tile([P, 1], F32)
+        nc.gpsimd.memset(warm[:], 0.0)
+        nc.scalar.activation(out=warm[:], in_=warm[:], func=ACT.Tanh)
+
+        identity = consts.tile([P, P], F32)
+        make_identity(nc, identity[:])
+        ones = consts.tile([P, P], BF16)
+        nc.gpsimd.memset(ones[:], 1.0)
+        bias_rows = consts.tile([P, GATES * H], BF16)
+        nc.gpsimd.memset(bias_rows[:], 0.0)
+
+        planes = weights.tile([P, SLOTS, GATES * H], U8, align_bytes=64)
+        for slot in range(SLOTS):
+            nc.vector.memset(planes[:, slot, :].bitcast(I32), 0)
+            first = slot * PLANES_PER_SLOT
+            for quadrant in range(4):
+                rows = slice(4 * quadrant, 4 * quadrant + 4)
+                if first < X_GROUPS:
+                    nc.sync.dma_start(
+                        out=planes[32 * quadrant : 32 * quadrant + 16, slot, :].bitcast(I32),
+                        in_=W_scales[first : first + PLANES_PER_SLOT, rows, :].bitcast(I32),
+                    )
+                else:
+                    nc.sync.dma_start(
+                        out=planes[32 * quadrant : 32 * quadrant + 4, slot, :].bitcast(I32),
+                        in_=R_scales[0, rows, :].bitcast(I32),
+                    )
+
+        act_rows = acts.tile([P, GROUPS * K_PASS], BF16)
+        for first in range(0, X_GROUPS, CHUNK):
+            columns = slice(first * K_PASS, (first + CHUNK) * K_PASS)
+            nc.sync.dma_start(out=act_rows[:, columns], in_=x_t[:, columns])
+        nc.sync.dma_start(out=act_rows[:, D : D + H], in_=h_prev[:, :])
+
+        nc.sync.dma_start(out=bias_rows[0:1, :], in_=b.rearrange("(o n) -> o n", o=1))
+        c_old = cell.tile([P, H], BF16)
+        nc.sync.dma_start(out=c_old[:], in_=c_prev[:, :])
+        n_old = cell.tile([P, H], BF16)
+        nc.sync.dma_start(out=n_old[:], in_=n_prev[:, :])
+
+        group_words = [W_words[g] for g in range(X_GROUPS)] + [R_words[0]]
+        words_zif = []
+        for g in range(GROUPS):
+            words = weights.tile([P, 3 * H], I32, name="words_zif%d" % g, align_bytes=64)
+            source = group_words[g][:, 0 : 3 * H, :].rearrange("p n t -> p (n t)")
+            nc.sync.dma_start(out=words[:], in_=source.bitcast(I32))
+            words_zif.append(words)
+        words_o = []
+        for g in range(GROUPS):
+            words = weights.tile([P, H], I32, name="words_o%d" % g, align_bytes=64)
+            source = group_words[g][:, 3 * H : 4 * H, :].rearrange("p n t -> p (n t)")
+            nc.sync.dma_start(out=words[:], in_=source.bitcast(I32))
+            words_o.append(words)
+
+        act_words = act_rows[:].bitcast(F32)
+        act_codes = acts.tile([P, GROUPS * P], U32, align_bytes=64)
+        act_scales = acts.tile([P, GROUPS * P], U8, align_bytes=64)
+        for first in range(0, GROUPS, CHUNK):
+            count = min(CHUNK, GROUPS - first)
+            grouped = stage.tile([P, count * K_PASS], BF16, tag="grouped", align_bytes=64)
+            grouped_words = grouped[:].bitcast(F32).rearrange("p (g m u) -> p g m u", m=P, u=2)
+            for bank, bank_first in enumerate(range(0, count, 2)):
+                in_bank = min(2, count - bank_first)
+                halves = work_psum.tile([P, in_bank, 2, P], F32, tag="work")
+                for j in range(in_bank):
+                    start_word = (first + bank_first + j) * WORDS_PER_GROUP
+                    for u in range(2):
+                        nc.tensor.transpose(
+                            halves[:, j, u, :],
+                            act_words[:, start_word + u : start_word + WORDS_PER_GROUP : 2],
+                            identity[:],
+                        )
+                target = grouped_words[:, bank_first : bank_first + in_bank, :, :]
+                if bank == 0:
+                    nc.vector.tensor_copy(out=target, in_=halves[:].rearrange("p g u m -> p g m u"))
+                else:
+                    nc.scalar.copy(out=target, in_=halves[:].rearrange("p g u m -> p g m u"))
+            columns = slice(first * P, (first + count) * P)
+            nc.vector.quantize_mx(
+                out=act_codes[:, columns].bitcast(FP8X4),
+                scales=act_scales[:, columns],
+                in_=grouped[:],
+            )
+
+        pre = cell.tile([P, GATES * H], F32)
+        for gate in range(GATES):
+            spread = work_psum.tile([P, H], F32, tag="work")
+            nc.tensor.matmul(
+                spread[:], lhsT=ones[:], rhs=bias_rows[:, gate_columns(gate)], start=True, stop=True
+            )
+            nc.scalar.copy(out=pre[:, gate_columns(gate)], in_=spread[:])
+
+        sums = [gate_psum.tile([P, H], F32, name="sums%d" % gate) for gate in range(GATES)]
+
+        def mx_pass(g, gate, words):
+            slot, plane_start = g // PLANES_PER_SLOT, 4 * (g % PLANES_PER_SLOT)
+            nc.tensor.matmul_mx(
+                out=sums[gate][:],
+                lhsT=act_codes[:, g * P : (g + 1) * P].bitcast(FP8X4),
+                lhsT_scale=act_scales[:, g * P : (g + 1) * P],
+                rhs=words.bitcast(FP8X4),
+                rhs_scale=planes[plane_start:P, slot, gate_columns(gate)],
+                start=(g == 0),
+                stop=(g == GROUPS - 1),
+            )
+
+        def add_sums(gate):
+            nc.vector.tensor_tensor(
+                out=pre[:, gate_columns(gate)],
+                in0=sums[gate][:],
+                in1=pre[:, gate_columns(gate)],
+                op=ALU.add,
+            )
+
+        for g in range(GROUPS):
+            for gate in (I, F, Z):
+                mx_pass(g, gate, words_zif[g][:, gate_columns(gate)])
+
+        add_sums(I)
+        exp_i = cell.tile([P, H], F32)
+        nc.scalar.activation(out=exp_i[:], in_=pre[:, gate_columns(I)], func=ACT.Exp)
+        add_sums(F)
+        tanh_f = cell.tile([P, H], F32)
+        nc.scalar.activation(out=tanh_f[:], in_=pre[:, gate_columns(F)], func=ACT.Tanh, scale=0.5)
+        add_sums(Z)
+        z_gate = cell.tile([P, H], F32)
+        nc.scalar.activation(out=z_gate[:], in_=pre[:, gate_columns(Z)], func=ACT.Tanh)
+
+        f_gate = cell.tile([P, H], F32)
+        nc.vector.tensor_scalar(
+            out=f_gate[:], in0=tanh_f[:], scalar1=0.5, scalar2=0.5, op0=ALU.mult, op1=ALU.add
+        )
+        f_n = cell.tile([P, H], F32)
+        nc.vector.tensor_tensor(out=f_n[:], in0=f_gate[:], in1=n_old[:], op=ALU.mult)
+        n_new = cell.tile([P, H], F32)
+        nc.vector.scalar_tensor_tensor(
+            out=n_new[:], in0=exp_i[:], scalar=50.0, in1=f_n[:], op0=ALU.min, op1=ALU.add
+        )
+        nc.sync.dma_start(out=out_2[:, :], in_=n_new[:])
+        f_c = cell.tile([P, H], F32)
+        nc.vector.tensor_tensor(out=f_c[:], in0=f_gate[:], in1=c_old[:], op=ALU.mult)
+        i_z = cell.tile([P, H], F32)
+        nc.vector.scalar_tensor_tensor(
+            out=i_z[:], in0=exp_i[:], scalar=50.0, in1=z_gate[:], op0=ALU.min, op1=ALU.mult
+        )
+        c_new = cell.tile([P, H], F32)
+        nc.vector.tensor_tensor(out=c_new[:], in0=f_c[:], in1=i_z[:], op=ALU.add)
+        nc.sync.dma_start(out=out_1[:, :], in_=c_new[:])
+        n_eps = cell.tile([P, H], F32)
+        nc.vector.tensor_scalar(out=n_eps[:], in0=n_new[:], scalar1=1e-6, scalar2=None, op0=ALU.add)
+        inverse = cell.tile([P, H], F32)
+        nc.vector.reciprocal(out=inverse[:], in_=n_eps[:])
+        half_ratio = cell.tile([P, H], F32)
+        nc.vector.scalar_tensor_tensor(
+            out=half_ratio[:], in0=c_new[:], scalar=0.5, in1=inverse[:], op0=ALU.mult, op1=ALU.mult
+        )
+
+        for g in range(GROUPS):
+            mx_pass(g, O, words_o[g][:])
+        add_sums(O)
+        tanh_o = cell.tile([P, H], F32)
+        nc.scalar.activation(out=tanh_o[:], in_=pre[:, gate_columns(O)], func=ACT.Tanh, scale=0.5)
+        h_new = cell.tile([P, H], F32)
+        nc.vector.scalar_tensor_tensor(
+            out=h_new[:], in0=tanh_o[:], scalar=1.0, in1=half_ratio[:], op0=ALU.add, op1=ALU.mult
+        )
+        nc.sync.dma_start(out=out_0[:, :], in_=h_new[:])

@@ -38,6 +38,7 @@ def tile_slstmcell_k_kernel(
 ):
     nc = tc.nc
     with ExitStack() as ctx:
+        ctx.enter_context(tc.manual_schedule())
         consts = ctx.enter_context(tc.tile_pool(name="consts", bufs=1))
         weights = ctx.enter_context(tc.tile_pool(name="weights", bufs=1))
         acts = ctx.enter_context(tc.tile_pool(name="acts", bufs=1))
@@ -47,15 +48,10 @@ def tile_slstmcell_k_kernel(
         work_psum = ctx.enter_context(tc.psum_pool(name="work_psum", bufs=4))
 
         warm = consts.tile([P, 1], F32)
-        nc.gpsimd.memset(warm[:], 0.0)
+        nc.vector.memset(warm[:], 0.0)
         nc.scalar.activation(out=warm[:], in_=warm[:], func=ACT.Tanh)
-
         identity = consts.tile([P, P], F32)
         make_identity(nc, identity[:])
-        ones = consts.tile([P, P], BF16)
-        nc.gpsimd.memset(ones[:], 1.0)
-        bias_rows = consts.tile([P, GATES * H], BF16)
-        nc.gpsimd.memset(bias_rows[:], 0.0)
 
         planes = weights.tile([P, SLOTS, GATES * H], U8, align_bytes=64)
         for slot in range(SLOTS):
@@ -64,15 +60,20 @@ def tile_slstmcell_k_kernel(
             for quadrant in range(4):
                 rows = slice(4 * quadrant, 4 * quadrant + 4)
                 if first < X_GROUPS:
-                    nc.sync.dma_start(
-                        out=planes[32 * quadrant : 32 * quadrant + 16, slot, :].bitcast(I32),
-                        in_=W_scales[first : first + PLANES_PER_SLOT, rows, :].bitcast(I32),
+                    nc.gpsimd.dma_start(
+                        out=planes[32 * quadrant : 32 * quadrant + 16, slot, :].bitcast(F32),
+                        in_=W_scales[first : first + PLANES_PER_SLOT, rows, :].bitcast(F32),
                     )
                 else:
-                    nc.sync.dma_start(
-                        out=planes[32 * quadrant : 32 * quadrant + 4, slot, :].bitcast(I32),
-                        in_=R_scales[0, rows, :].bitcast(I32),
+                    nc.gpsimd.dma_start(
+                        out=planes[32 * quadrant : 32 * quadrant + 4, slot, :].bitcast(F32),
+                        in_=R_scales[0, rows, :].bitcast(F32),
                     )
+
+        ones = consts.tile([P, P], BF16)
+        nc.vector.memset(ones[:], 1.0)
+        bias_rows = consts.tile([P, GATES * H], BF16)
+        nc.vector.memset(bias_rows[:], 0.0)
 
         act_rows = acts.tile([P, GROUPS * K_PASS], BF16)
         for first in range(0, X_GROUPS, CHUNK):
@@ -174,25 +175,23 @@ def tile_slstmcell_k_kernel(
         z_gate = cell.tile([P, H], F32)
         nc.scalar.activation(out=z_gate[:], in_=pre[:, gate_columns(Z)], func=ACT.Tanh)
 
+        i_gate = cell.tile([P, H], F32)
+        nc.vector.tensor_scalar(out=i_gate[:], in0=exp_i[:], scalar1=50.0, scalar2=None, op0=ALU.min)
         f_gate = cell.tile([P, H], F32)
         nc.vector.tensor_scalar(
             out=f_gate[:], in0=tanh_f[:], scalar1=0.5, scalar2=0.5, op0=ALU.mult, op1=ALU.add
         )
+        f_c = cell.tile([P, H], F32)
+        nc.gpsimd.tensor_tensor(out=f_c[:], in0=f_gate[:], in1=c_old[:], op=ALU.mult)
+        i_z = cell.tile([P, H], F32)
+        nc.gpsimd.tensor_tensor(out=i_z[:], in0=i_gate[:], in1=z_gate[:], op=ALU.mult)
+        c_new = cell.tile([P, H], F32)
+        nc.gpsimd.tensor_tensor(out=c_new[:], in0=f_c[:], in1=i_z[:], op=ALU.add)
         f_n = cell.tile([P, H], F32)
         nc.vector.tensor_tensor(out=f_n[:], in0=f_gate[:], in1=n_old[:], op=ALU.mult)
         n_new = cell.tile([P, H], F32)
-        nc.vector.scalar_tensor_tensor(
-            out=n_new[:], in0=exp_i[:], scalar=50.0, in1=f_n[:], op0=ALU.min, op1=ALU.add
-        )
+        nc.vector.tensor_tensor(out=n_new[:], in0=f_n[:], in1=i_gate[:], op=ALU.add)
         nc.sync.dma_start(out=out_2[:, :], in_=n_new[:])
-        f_c = cell.tile([P, H], F32)
-        nc.vector.tensor_tensor(out=f_c[:], in0=f_gate[:], in1=c_old[:], op=ALU.mult)
-        i_z = cell.tile([P, H], F32)
-        nc.vector.scalar_tensor_tensor(
-            out=i_z[:], in0=exp_i[:], scalar=50.0, in1=z_gate[:], op0=ALU.min, op1=ALU.mult
-        )
-        c_new = cell.tile([P, H], F32)
-        nc.vector.tensor_tensor(out=c_new[:], in0=f_c[:], in1=i_z[:], op=ALU.add)
         nc.sync.dma_start(out=out_1[:, :], in_=c_new[:])
         n_eps = cell.tile([P, H], F32)
         nc.vector.tensor_scalar(out=n_eps[:], in0=n_new[:], scalar1=1e-6, scalar2=None, op0=ALU.add)

@@ -25,6 +25,8 @@ WORDS_PER_GROUP = K_PASS // 2
 CHUNK = 4
 PLANES_PER_SLOT = 4
 SLOTS = (GROUPS + PLANES_PER_SLOT - 1) // PLANES_PER_SLOT
+LATE_GROUPS = 8
+O_PARTS = 2
 
 FLOPS = 2 * P * (D + H) * GATES * H
 
@@ -87,19 +89,19 @@ def tile_slstmcell_k_kernel(
         n_old = cell.tile([P, H], BF16)
         nc.sync.dma_start(out=n_old[:], in_=n_prev[:, :])
 
+        early = range(GROUPS - LATE_GROUPS)
+        late = range(GROUPS - LATE_GROUPS, GROUPS)
+        pieces = [(g, Z, 3) for g in early]
+        pieces += [(g, I, 2) for g in late]
+        pieces += [(g, Z, 1) for g in late]
+        pieces += [(g, O, 1) for g in range(GROUPS)]
         group_words = [W_words[g] for g in range(X_GROUPS)] + [R_words[0]]
-        words_zif = []
-        for g in range(GROUPS):
-            words = weights.tile([P, 3 * H], I32, name="words_zif%d" % g, align_bytes=64)
-            source = group_words[g][:, 0 : 3 * H, :].rearrange("p n t -> p (n t)")
-            nc.sync.dma_start(out=words[:], in_=source.bitcast(I32))
-            words_zif.append(words)
-        words_o = []
-        for g in range(GROUPS):
-            words = weights.tile([P, H], I32, name="words_o%d" % g, align_bytes=64)
-            source = group_words[g][:, 3 * H : 4 * H, :].rearrange("p n t -> p (n t)")
-            nc.sync.dma_start(out=words[:], in_=source.bitcast(I32))
-            words_o.append(words)
+        piece_words = []
+        for g, first_gate, gates in pieces:
+            words = weights.tile([P, gates * H], I32, name="words%d_%d" % (g, first_gate), align_bytes=64)
+            source = group_words[g][:, first_gate * H : (first_gate + gates) * H, :]
+            nc.sync.dma_start(out=words[:], in_=source.rearrange("p n t -> p (n t)").bitcast(I32))
+            piece_words.append(words)
 
         act_words = act_rows[:].bitcast(F32)
         act_codes = acts.tile([P, GROUPS * P], U32, align_bytes=64)
@@ -110,20 +112,20 @@ def tile_slstmcell_k_kernel(
             grouped_words = grouped[:].bitcast(F32).rearrange("p (g m u) -> p g m u", m=P, u=2)
             for bank, bank_first in enumerate(range(0, count, 2)):
                 in_bank = min(2, count - bank_first)
-                halves = work_psum.tile([P, in_bank, 2, P], F32, tag="work")
+                transposed = work_psum.tile([P, in_bank, 2, P], F32, tag="work")
                 for j in range(in_bank):
                     start_word = (first + bank_first + j) * WORDS_PER_GROUP
                     for u in range(2):
                         nc.tensor.transpose(
-                            halves[:, j, u, :],
+                            transposed[:, j, u, :],
                             act_words[:, start_word + u : start_word + WORDS_PER_GROUP : 2],
                             identity[:],
                         )
                 target = grouped_words[:, bank_first : bank_first + in_bank, :, :]
                 if bank == 0:
-                    nc.vector.tensor_copy(out=target, in_=halves[:].rearrange("p g u m -> p g m u"))
+                    nc.vector.tensor_copy(out=target, in_=transposed[:].rearrange("p g u m -> p g m u"))
                 else:
-                    nc.scalar.copy(out=target, in_=halves[:].rearrange("p g u m -> p g m u"))
+                    nc.scalar.copy(out=target, in_=transposed[:].rearrange("p g u m -> p g m u"))
             columns = slice(first * P, (first + count) * P)
             nc.vector.quantize_mx(
                 out=act_codes[:, columns].bitcast(FP8X4),
@@ -131,13 +133,13 @@ def tile_slstmcell_k_kernel(
                 in_=grouped[:],
             )
 
-        pre = cell.tile([P, GATES * H], F32)
+        pre = cell.tile([P, GATES, H], F32)
         for gate in range(GATES):
             spread = work_psum.tile([P, H], F32, tag="work")
             nc.tensor.matmul(
                 spread[:], lhsT=ones[:], rhs=bias_rows[:, gate_columns(gate)], start=True, stop=True
             )
-            nc.scalar.copy(out=pre[:, gate_columns(gate)], in_=spread[:])
+            nc.scalar.copy(out=pre[:, gate, :], in_=spread[:])
 
         sums = [gate_psum.tile([P, H], F32, name="sums%d" % gate) for gate in range(GATES)]
 
@@ -153,62 +155,73 @@ def tile_slstmcell_k_kernel(
                 stop=(g == GROUPS - 1),
             )
 
-        def add_sums(gate):
+        for (g, first_gate, gates), words in zip(pieces, piece_words):
+            for j in range(gates):
+                mx_pass(g, first_gate + j, words[:, j * H : (j + 1) * H])
+
+        def add_sums(gate, columns):
             nc.vector.tensor_tensor(
-                out=pre[:, gate_columns(gate)],
-                in0=sums[gate][:],
-                in1=pre[:, gate_columns(gate)],
+                out=pre[:, gate, columns],
+                in0=sums[gate][:, columns],
+                in1=pre[:, gate, columns],
                 op=ALU.add,
             )
 
-        for g in range(GROUPS):
-            for gate in (I, F, Z):
-                mx_pass(g, gate, words_zif[g][:, gate_columns(gate)])
+        whole = slice(0, H)
 
-        add_sums(I)
+        add_sums(I, whole)
         exp_i = cell.tile([P, H], F32)
-        nc.scalar.activation(out=exp_i[:], in_=pre[:, gate_columns(I)], func=ACT.Exp)
-        add_sums(F)
+        nc.scalar.activation(out=exp_i[:], in_=pre[:, I, :], func=ACT.Exp)
+        add_sums(F, whole)
         tanh_f = cell.tile([P, H], F32)
-        nc.scalar.activation(out=tanh_f[:], in_=pre[:, gate_columns(F)], func=ACT.Tanh, scale=0.5)
-        add_sums(Z)
-        z_gate = cell.tile([P, H], F32)
-        nc.scalar.activation(out=z_gate[:], in_=pre[:, gate_columns(Z)], func=ACT.Tanh)
-
+        nc.scalar.activation(out=tanh_f[:], in_=pre[:, F, :], func=ACT.Tanh, scale=0.5)
         i_gate = cell.tile([P, H], F32)
         nc.vector.tensor_scalar(out=i_gate[:], in0=exp_i[:], scalar1=50.0, scalar2=None, op0=ALU.min)
         f_gate = cell.tile([P, H], F32)
         nc.vector.tensor_scalar(
             out=f_gate[:], in0=tanh_f[:], scalar1=0.5, scalar2=0.5, op0=ALU.mult, op1=ALU.add
         )
-        f_c = cell.tile([P, H], F32)
-        nc.gpsimd.tensor_tensor(out=f_c[:], in0=f_gate[:], in1=c_old[:], op=ALU.mult)
-        i_z = cell.tile([P, H], F32)
-        nc.gpsimd.tensor_tensor(out=i_z[:], in0=i_gate[:], in1=z_gate[:], op=ALU.mult)
-        c_new = cell.tile([P, H], F32)
-        nc.gpsimd.tensor_tensor(out=c_new[:], in0=f_c[:], in1=i_z[:], op=ALU.add)
         f_n = cell.tile([P, H], F32)
         nc.vector.tensor_tensor(out=f_n[:], in0=f_gate[:], in1=n_old[:], op=ALU.mult)
         n_new = cell.tile([P, H], F32)
         nc.vector.tensor_tensor(out=n_new[:], in0=f_n[:], in1=i_gate[:], op=ALU.add)
         nc.sync.dma_start(out=out_2[:, :], in_=n_new[:])
-        nc.sync.dma_start(out=out_1[:, :], in_=c_new[:])
         n_eps = cell.tile([P, H], F32)
         nc.vector.tensor_scalar(out=n_eps[:], in0=n_new[:], scalar1=1e-6, scalar2=None, op0=ALU.add)
+
+        add_sums(Z, whole)
+        z_gate = cell.tile([P, H], F32)
+        nc.scalar.activation(out=z_gate[:], in_=pre[:, Z, :], func=ACT.Tanh)
         inverse = cell.tile([P, H], F32)
         nc.vector.reciprocal(out=inverse[:], in_=n_eps[:])
+        f_c = cell.tile([P, H], F32)
+        nc.vector.tensor_tensor(out=f_c[:], in0=f_gate[:], in1=c_old[:], op=ALU.mult)
+        i_z = cell.tile([P, H], F32)
+        nc.vector.tensor_tensor(out=i_z[:], in0=i_gate[:], in1=z_gate[:], op=ALU.mult)
+        c_new = cell.tile([P, H], F32)
+        nc.vector.tensor_tensor(out=c_new[:], in0=f_c[:], in1=i_z[:], op=ALU.add)
+        nc.sync.dma_start(out=out_1[:, :], in_=c_new[:])
         half_ratio = cell.tile([P, H], F32)
         nc.vector.scalar_tensor_tensor(
             out=half_ratio[:], in0=c_new[:], scalar=0.5, in1=inverse[:], op0=ALU.mult, op1=ALU.mult
         )
 
-        for g in range(GROUPS):
-            mx_pass(g, O, words_o[g][:])
-        add_sums(O)
+        parts_of_o = [slice(j * H // O_PARTS, (j + 1) * H // O_PARTS) for j in range(O_PARTS)]
         tanh_o = cell.tile([P, H], F32)
-        nc.scalar.activation(out=tanh_o[:], in_=pre[:, gate_columns(O)], func=ACT.Tanh, scale=0.5)
         h_new = cell.tile([P, H], F32)
-        nc.vector.scalar_tensor_tensor(
-            out=h_new[:], in0=tanh_o[:], scalar=1.0, in1=half_ratio[:], op0=ALU.add, op1=ALU.mult
-        )
-        nc.sync.dma_start(out=out_0[:, :], in_=h_new[:])
+        for columns in parts_of_o:
+            add_sums(O, columns)
+        for columns in parts_of_o:
+            nc.scalar.activation(
+                out=tanh_o[:, columns], in_=pre[:, O, columns], func=ACT.Tanh, scale=0.5
+            )
+        for columns in parts_of_o:
+            nc.vector.scalar_tensor_tensor(
+                out=h_new[:, columns],
+                in0=tanh_o[:, columns],
+                scalar=1.0,
+                in1=half_ratio[:, columns],
+                op0=ALU.add,
+                op1=ALU.mult,
+            )
+            nc.sync.dma_start(out=out_0[:, columns], in_=h_new[:, columns])

@@ -25,7 +25,8 @@ WORDS_PER_GROUP = K_PASS // 2
 CHUNK = 4
 PLANES_PER_SLOT = 4
 SLOTS = (GROUPS + PLANES_PER_SLOT - 1) // PLANES_PER_SLOT
-LATE_GROUPS = 8
+LATE_Z = 4
+LATE_O = 12
 O_PARTS = 2
 
 FLOPS = 2 * P * (D + H) * GATES * H
@@ -89,12 +90,13 @@ def tile_slstmcell_k_kernel(
         n_old = cell.tile([P, H], BF16)
         nc.sync.dma_start(out=n_old[:], in_=n_prev[:, :])
 
-        early = range(GROUPS - LATE_GROUPS)
-        late = range(GROUPS - LATE_GROUPS, GROUPS)
-        pieces = [(g, Z, 3) for g in early]
-        pieces += [(g, I, 2) for g in late]
-        pieces += [(g, Z, 1) for g in late]
-        pieces += [(g, O, 1) for g in range(GROUPS)]
+        late_o = range(GROUPS - LATE_O, GROUPS)
+        late_z = range(GROUPS - LATE_Z, GROUPS)
+        pieces = [(g, Z, 4) for g in range(GROUPS - LATE_O)]
+        pieces += [(g, Z, 3) for g in range(GROUPS - LATE_O, GROUPS - LATE_Z)]
+        pieces += [(g, I, 2) for g in late_z]
+        pieces += [(g, Z, 1) for g in late_z]
+        pieces += [(g, O, 1) for g in late_o]
         group_words = [W_words[g] for g in range(X_GROUPS)] + [R_words[0]]
         piece_words = []
         for g, first_gate, gates in pieces:
@@ -169,35 +171,42 @@ def tile_slstmcell_k_kernel(
 
         whole = slice(0, H)
 
+        half_n = cell.tile([P, H], F32)
+        nc.vector.tensor_scalar(out=half_n[:], in0=n_old[:], scalar1=0.5, scalar2=None, op0=ALU.mult)
+        half_c = cell.tile([P, H], F32)
+        nc.vector.tensor_scalar(out=half_c[:], in0=c_old[:], scalar1=0.5, scalar2=None, op0=ALU.mult)
+
         add_sums(I, whole)
         exp_i = cell.tile([P, H], F32)
         nc.scalar.activation(out=exp_i[:], in_=pre[:, I, :], func=ACT.Exp)
         add_sums(F, whole)
         tanh_f = cell.tile([P, H], F32)
         nc.scalar.activation(out=tanh_f[:], in_=pre[:, F, :], func=ACT.Tanh, scale=0.5)
-        i_gate = cell.tile([P, H], F32)
-        nc.vector.tensor_scalar(out=i_gate[:], in0=exp_i[:], scalar1=50.0, scalar2=None, op0=ALU.min)
-        f_gate = cell.tile([P, H], F32)
-        nc.vector.tensor_scalar(
-            out=f_gate[:], in0=tanh_f[:], scalar1=0.5, scalar2=0.5, op0=ALU.mult, op1=ALU.add
-        )
         f_n = cell.tile([P, H], F32)
-        nc.vector.tensor_tensor(out=f_n[:], in0=f_gate[:], in1=n_old[:], op=ALU.mult)
+        nc.vector.scalar_tensor_tensor(
+            out=f_n[:], in0=tanh_f[:], scalar=1.0, in1=half_n[:], op0=ALU.add, op1=ALU.mult
+        )
         n_new = cell.tile([P, H], F32)
-        nc.vector.tensor_tensor(out=n_new[:], in0=f_n[:], in1=i_gate[:], op=ALU.add)
+        nc.vector.scalar_tensor_tensor(
+            out=n_new[:], in0=exp_i[:], scalar=50.0, in1=f_n[:], op0=ALU.min, op1=ALU.add
+        )
         nc.sync.dma_start(out=out_2[:, :], in_=n_new[:])
         n_eps = cell.tile([P, H], F32)
         nc.vector.tensor_scalar(out=n_eps[:], in0=n_new[:], scalar1=1e-6, scalar2=None, op0=ALU.add)
 
+        f_c = cell.tile([P, H], F32)
+        nc.vector.scalar_tensor_tensor(
+            out=f_c[:], in0=tanh_f[:], scalar=1.0, in1=half_c[:], op0=ALU.add, op1=ALU.mult
+        )
         add_sums(Z, whole)
         z_gate = cell.tile([P, H], F32)
         nc.scalar.activation(out=z_gate[:], in_=pre[:, Z, :], func=ACT.Tanh)
         inverse = cell.tile([P, H], F32)
         nc.vector.reciprocal(out=inverse[:], in_=n_eps[:])
-        f_c = cell.tile([P, H], F32)
-        nc.vector.tensor_tensor(out=f_c[:], in0=f_gate[:], in1=c_old[:], op=ALU.mult)
         i_z = cell.tile([P, H], F32)
-        nc.vector.tensor_tensor(out=i_z[:], in0=i_gate[:], in1=z_gate[:], op=ALU.mult)
+        nc.vector.scalar_tensor_tensor(
+            out=i_z[:], in0=exp_i[:], scalar=50.0, in1=z_gate[:], op0=ALU.min, op1=ALU.mult
+        )
         c_new = cell.tile([P, H], F32)
         nc.vector.tensor_tensor(out=c_new[:], in0=f_c[:], in1=i_z[:], op=ALU.add)
         nc.sync.dma_start(out=out_1[:, :], in_=c_new[:])

@@ -25,8 +25,19 @@ WORDS_PER_GROUP = K_PASS // 2
 CHUNK = 4
 PLANES_PER_SLOT = 4
 SLOTS = (GROUPS + PLANES_PER_SLOT - 1) // PLANES_PER_SLOT
-LATE_Z = 4
-LATE_O = 12
+LOADS = (
+    (0, 4, Z, 3),
+    (4, 4, Z, 3),
+    (X_GROUPS, 1, Z, 4),
+    (8, 4, Z, 3),
+    (12, 3, I, 2),
+    (15, 1, I, 2),
+    (12, 4, Z, 1),
+    (0, 5, O, 1),
+    (5, 5, O, 1),
+    (10, 4, O, 1),
+    (14, 2, O, 1),
+)
 O_PARTS = 2
 
 FLOPS = 2 * P * (D + H) * GATES * H
@@ -90,20 +101,17 @@ def tile_slstmcell_k_kernel(
         n_old = cell.tile([P, H], BF16)
         nc.sync.dma_start(out=n_old[:], in_=n_prev[:, :])
 
-        late_o = range(GROUPS - LATE_O, GROUPS)
-        late_z = range(GROUPS - LATE_Z, GROUPS)
-        pieces = [(g, Z, 4) for g in range(GROUPS - LATE_O)]
-        pieces += [(g, Z, 3) for g in range(GROUPS - LATE_O, GROUPS - LATE_Z)]
-        pieces += [(g, I, 2) for g in late_z]
-        pieces += [(g, Z, 1) for g in late_z]
-        pieces += [(g, O, 1) for g in late_o]
-        group_words = [W_words[g] for g in range(X_GROUPS)] + [R_words[0]]
-        piece_words = []
-        for g, first_gate, gates in pieces:
-            words = weights.tile([P, gates * H], I32, name="words%d_%d" % (g, first_gate), align_bytes=64)
-            source = group_words[g][:, first_gate * H : (first_gate + gates) * H, :]
-            nc.sync.dma_start(out=words[:], in_=source.rearrange("p n t -> p (n t)").bitcast(I32))
-            piece_words.append(words)
+        passes = []
+        for first_group, groups, first_gate, gates in LOADS:
+            words = weights.tile(
+                [P, groups, gates * H], I32, name="words%d_%d" % (first_group, first_gate), align_bytes=64
+            )
+            tensor, start = (W_words, first_group) if first_group < X_GROUPS else (R_words, 0)
+            source = tensor[start : start + groups, :, first_gate * H : (first_gate + gates) * H, :]
+            nc.sync.dma_start(out=words[:], in_=source.rearrange("g p n t -> p g (n t)").bitcast(I32))
+            for j in range(groups):
+                for k in reversed(range(gates)):
+                    passes.append((first_group + j, first_gate + k, words[:, j, k * H : (k + 1) * H]))
 
         act_words = act_rows[:].bitcast(F32)
         act_codes = acts.tile([P, GROUPS * P], U32, align_bytes=64)
@@ -145,7 +153,7 @@ def tile_slstmcell_k_kernel(
 
         sums = [gate_psum.tile([P, H], F32, name="sums%d" % gate) for gate in range(GATES)]
 
-        def mx_pass(g, gate, words):
+        def mx_pass(g, gate, words, start, stop):
             slot, plane_start = g // PLANES_PER_SLOT, 4 * (g % PLANES_PER_SLOT)
             nc.tensor.matmul_mx(
                 out=sums[gate][:],
@@ -153,13 +161,15 @@ def tile_slstmcell_k_kernel(
                 lhsT_scale=act_scales[:, g * P : (g + 1) * P],
                 rhs=words.bitcast(FP8X4),
                 rhs_scale=planes[plane_start:P, slot, gate_columns(gate)],
-                start=(g == 0),
-                stop=(g == GROUPS - 1),
+                start=start,
+                stop=stop,
             )
 
-        for (g, first_gate, gates), words in zip(pieces, piece_words):
-            for j in range(gates):
-                mx_pass(g, first_gate + j, words[:, j * H : (j + 1) * H])
+        gate_order = [gate for g, gate, words in passes]
+        for k, (g, gate, words) in enumerate(passes):
+            mx_pass(
+                g, gate, words, start=(gate not in gate_order[:k]), stop=(gate not in gate_order[k + 1 :])
+            )
 
         def add_sums(gate, columns):
             nc.vector.tensor_tensor(
@@ -176,12 +186,12 @@ def tile_slstmcell_k_kernel(
         half_c = cell.tile([P, H], F32)
         nc.vector.tensor_scalar(out=half_c[:], in0=c_old[:], scalar1=0.5, scalar2=None, op0=ALU.mult)
 
-        add_sums(I, whole)
-        exp_i = cell.tile([P, H], F32)
-        nc.scalar.activation(out=exp_i[:], in_=pre[:, I, :], func=ACT.Exp)
         add_sums(F, whole)
         tanh_f = cell.tile([P, H], F32)
         nc.scalar.activation(out=tanh_f[:], in_=pre[:, F, :], func=ACT.Tanh, scale=0.5)
+        add_sums(I, whole)
+        exp_i = cell.tile([P, H], F32)
+        nc.scalar.activation(out=exp_i[:], in_=pre[:, I, :], func=ACT.Exp)
         f_n = cell.tile([P, H], F32)
         nc.vector.scalar_tensor_tensor(
             out=f_n[:], in0=tanh_f[:], scalar=1.0, in1=half_n[:], op0=ALU.add, op1=ALU.mult

@@ -25,20 +25,23 @@ WORDS_PER_GROUP = K_PASS // 2
 CHUNK = 4
 PLANES_PER_SLOT = 4
 SLOTS = (GROUPS + PLANES_PER_SLOT - 1) // PLANES_PER_SLOT
+SEG_Z, SEG_I, SEG_F = (0, 512), (512, 512), (1024, 512)
+SEG_OA, SEG_OB, SEG_OC = (1536, 256), (1792, 128), (1920, 128)
+SEGMENTS = (SEG_F, SEG_I, SEG_Z, SEG_OA, SEG_OB, SEG_OC)
 LOADS = (
-    (0, 4, Z, 3),
-    (4, 4, Z, 3),
-    (X_GROUPS, 1, Z, 4),
-    (8, 4, Z, 3),
-    (12, 3, I, 2),
-    (15, 1, I, 2),
-    (12, 4, Z, 1),
-    (0, 5, O, 1),
-    (5, 5, O, 1),
-    (10, 4, O, 1),
-    (14, 2, O, 1),
+    (0, 4, 0, 1536),
+    (4, 4, 0, 1536),
+    (8, 4, 512, 1024),
+    (X_GROUPS, 1, 0, 2048),
+    (12, 3, 512, 1024),
+    (15, 1, 512, 1024),
+    (8, 8, 0, 512),
+    (0, 16, 1536, 256),
+    (0, 16, 1792, 128),
+    (0, 8, 1920, 128),
+    (8, 5, 1920, 128),
+    (13, 3, 1920, 128),
 )
-O_PARTS = 2
 
 FLOPS = 2 * P * (D + H) * GATES * H
 
@@ -102,16 +105,18 @@ def tile_slstmcell_k_kernel(
         nc.sync.dma_start(out=n_old[:], in_=n_prev[:, :])
 
         passes = []
-        for first_group, groups, first_gate, gates in LOADS:
+        for first_group, groups, first_column, columns in LOADS:
             words = weights.tile(
-                [P, groups, gates * H], I32, name="words%d_%d" % (first_group, first_gate), align_bytes=64
+                [P, groups, columns], I32, name="words%d_%d" % (first_group, first_column), align_bytes=64
             )
             tensor, start = (W_words, first_group) if first_group < X_GROUPS else (R_words, 0)
-            source = tensor[start : start + groups, :, first_gate * H : (first_gate + gates) * H, :]
+            source = tensor[start : start + groups, :, first_column : first_column + columns, :]
             nc.sync.dma_start(out=words[:], in_=source.rearrange("g p n t -> p g (n t)").bitcast(I32))
             for j in range(groups):
-                for k in reversed(range(gates)):
-                    passes.append((first_group + j, first_gate + k, words[:, j, k * H : (k + 1) * H]))
+                for segment in SEGMENTS:
+                    offset = segment[0] - first_column
+                    if 0 <= offset < columns:
+                        passes.append((first_group + j, segment, words[:, j, offset : offset + segment[1]]))
 
         act_words = act_rows[:].bitcast(F32)
         act_codes = acts.tile([P, GROUPS * P], U32, align_bytes=64)
@@ -143,55 +148,52 @@ def tile_slstmcell_k_kernel(
                 in_=grouped[:],
             )
 
-        pre = cell.tile([P, GATES, H], F32)
+        pre = cell.tile([P, GATES * H], F32)
         for gate in range(GATES):
             spread = work_psum.tile([P, H], F32, tag="work")
             nc.tensor.matmul(
                 spread[:], lhsT=ones[:], rhs=bias_rows[:, gate_columns(gate)], start=True, stop=True
             )
-            nc.scalar.copy(out=pre[:, gate, :], in_=spread[:])
+            nc.scalar.copy(out=pre[:, gate_columns(gate)], in_=spread[:])
 
-        sums = [gate_psum.tile([P, H], F32, name="sums%d" % gate) for gate in range(GATES)]
+        sums = {}
+        for segment in SEGMENTS:
+            if segment in (SEG_OB, SEG_OC):
+                sums[segment] = work_psum.tile([P, H], F32, name="sums%d" % segment[0], tag="work")
+            else:
+                sums[segment] = gate_psum.tile([P, H], F32, name="sums%d" % segment[0])
 
-        def mx_pass(g, gate, words, start, stop):
+        order = [segment for g, segment, words in passes]
+        for k, (g, segment, words) in enumerate(passes):
             slot, plane_start = g // PLANES_PER_SLOT, 4 * (g % PLANES_PER_SLOT)
+            first_column, columns = segment
             nc.tensor.matmul_mx(
-                out=sums[gate][:],
+                out=sums[segment][:, 0:columns],
                 lhsT=act_codes[:, g * P : (g + 1) * P].bitcast(FP8X4),
                 lhsT_scale=act_scales[:, g * P : (g + 1) * P],
                 rhs=words.bitcast(FP8X4),
-                rhs_scale=planes[plane_start:P, slot, gate_columns(gate)],
-                start=start,
-                stop=stop,
+                rhs_scale=planes[plane_start:P, slot, first_column : first_column + columns],
+                start=(segment not in order[:k]),
+                stop=(segment not in order[k + 1 :]),
             )
 
-        gate_order = [gate for g, gate, words in passes]
-        for k, (g, gate, words) in enumerate(passes):
-            mx_pass(
-                g, gate, words, start=(gate not in gate_order[:k]), stop=(gate not in gate_order[k + 1 :])
-            )
-
-        def add_sums(gate, columns):
-            nc.vector.tensor_tensor(
-                out=pre[:, gate, columns],
-                in0=sums[gate][:, columns],
-                in1=pre[:, gate, columns],
-                op=ALU.add,
-            )
-
-        whole = slice(0, H)
+        def add_sums(segment):
+            first_column, columns = segment
+            values = pre[:, first_column : first_column + columns]
+            nc.vector.tensor_tensor(out=values, in0=sums[segment][:, 0:columns], in1=values, op=ALU.add)
+            return values
 
         half_n = cell.tile([P, H], F32)
         nc.vector.tensor_scalar(out=half_n[:], in0=n_old[:], scalar1=0.5, scalar2=None, op0=ALU.mult)
         half_c = cell.tile([P, H], F32)
         nc.vector.tensor_scalar(out=half_c[:], in0=c_old[:], scalar1=0.5, scalar2=None, op0=ALU.mult)
 
-        add_sums(F, whole)
+        pre_f = add_sums(SEG_F)
         tanh_f = cell.tile([P, H], F32)
-        nc.scalar.activation(out=tanh_f[:], in_=pre[:, F, :], func=ACT.Tanh, scale=0.5)
-        add_sums(I, whole)
+        nc.scalar.activation(out=tanh_f[:], in_=pre_f, func=ACT.Tanh, scale=0.5)
+        pre_i = add_sums(SEG_I)
         exp_i = cell.tile([P, H], F32)
-        nc.scalar.activation(out=exp_i[:], in_=pre[:, I, :], func=ACT.Exp)
+        nc.scalar.activation(out=exp_i[:], in_=pre_i, func=ACT.Exp)
         f_n = cell.tile([P, H], F32)
         nc.vector.scalar_tensor_tensor(
             out=f_n[:], in0=tanh_f[:], scalar=1.0, in1=half_n[:], op0=ALU.add, op1=ALU.mult
@@ -208,11 +210,11 @@ def tile_slstmcell_k_kernel(
         nc.vector.scalar_tensor_tensor(
             out=f_c[:], in0=tanh_f[:], scalar=1.0, in1=half_c[:], op0=ALU.add, op1=ALU.mult
         )
-        add_sums(Z, whole)
-        z_gate = cell.tile([P, H], F32)
-        nc.scalar.activation(out=z_gate[:], in_=pre[:, Z, :], func=ACT.Tanh)
         inverse = cell.tile([P, H], F32)
         nc.vector.reciprocal(out=inverse[:], in_=n_eps[:])
+        pre_z = add_sums(SEG_Z)
+        z_gate = cell.tile([P, H], F32)
+        nc.scalar.activation(out=z_gate[:], in_=pre_z, func=ACT.Tanh)
         i_z = cell.tile([P, H], F32)
         nc.vector.scalar_tensor_tensor(
             out=i_z[:], in0=exp_i[:], scalar=50.0, in1=z_gate[:], op0=ALU.min, op1=ALU.mult
@@ -225,16 +227,16 @@ def tile_slstmcell_k_kernel(
             out=half_ratio[:], in0=c_new[:], scalar=0.5, in1=inverse[:], op0=ALU.mult, op1=ALU.mult
         )
 
-        parts_of_o = [slice(j * H // O_PARTS, (j + 1) * H // O_PARTS) for j in range(O_PARTS)]
         tanh_o = cell.tile([P, H], F32)
         h_new = cell.tile([P, H], F32)
-        for columns in parts_of_o:
-            add_sums(O, columns)
-        for columns in parts_of_o:
-            nc.scalar.activation(
-                out=tanh_o[:, columns], in_=pre[:, O, columns], func=ACT.Tanh, scale=0.5
-            )
-        for columns in parts_of_o:
+        for segments in ((SEG_OA, SEG_OB), (SEG_OC,)):
+            for segment in segments:
+                columns = slice(segment[0] - O * H, segment[0] - O * H + segment[1])
+                nc.scalar.activation(
+                    out=tanh_o[:, columns], in_=add_sums(segment), func=ACT.Tanh, scale=0.5
+                )
+            first_column = segments[0][0] - O * H
+            columns = slice(first_column, first_column + sum(width for start, width in segments))
             nc.vector.scalar_tensor_tensor(
                 out=h_new[:, columns],
                 in0=tanh_o[:, columns],

@@ -24,6 +24,7 @@ GATES = 4
 WORDS_PER_GROUP = K_PASS // 2
 CHUNK = 4
 PLANES_PER_SLOT = 4
+SYNC_SLOTS = 2
 SLOTS = (GROUPS + PLANES_PER_SLOT - 1) // PLANES_PER_SLOT
 SEG_Z, SEG_I, SEG_F = (0, 512), (512, 512), (1024, 512)
 SEG_OA, SEG_OB, SEG_OC = (1536, 256), (1792, 128), (1920, 128)
@@ -32,8 +33,8 @@ LOADS = (
     (0, 4, 0, 1536),
     (4, 4, 0, 1536),
     (8, 4, 512, 1024),
-    (X_GROUPS, 1, 0, 2048),
     (12, 3, 512, 1024),
+    (X_GROUPS, 1, 0, 2048),
     (15, 1, 512, 1024),
     (8, 8, 0, 512),
     (0, 16, 1536, 256),
@@ -73,19 +74,22 @@ def tile_slstmcell_k_kernel(
         planes = weights.tile([P, SLOTS, GATES * H], U8, align_bytes=64)
         for slot in range(SLOTS):
             nc.vector.memset(planes[:, slot, :].bitcast(I32), 0)
+
+        def load_planes(queue, slot, quadrant, dtype):
+            rows = slice(4 * quadrant, 4 * quadrant + 4)
             first = slot * PLANES_PER_SLOT
-            for quadrant in range(4):
-                rows = slice(4 * quadrant, 4 * quadrant + 4)
-                if first < X_GROUPS:
-                    nc.gpsimd.dma_start(
-                        out=planes[32 * quadrant : 32 * quadrant + 16, slot, :].bitcast(F32),
-                        in_=W_scales[first : first + PLANES_PER_SLOT, rows, :].bitcast(F32),
-                    )
-                else:
-                    nc.gpsimd.dma_start(
-                        out=planes[32 * quadrant : 32 * quadrant + 4, slot, :].bitcast(F32),
-                        in_=R_scales[0, rows, :].bitcast(F32),
-                    )
+            groups = min(PLANES_PER_SLOT, GROUPS - first)
+            source = W_scales[first : first + groups] if first < X_GROUPS else R_scales
+            queue.dma_start(
+                out=planes[32 * quadrant : 32 * quadrant + 4 * groups, slot, :].bitcast(dtype),
+                in_=source[:, rows, :].bitcast(dtype),
+            )
+
+        large = [(slot, quadrant) for slot in range(SYNC_SLOTS, SLOTS - 1) for quadrant in range(4)]
+        for quadrant in range(4):
+            load_planes(nc.gpsimd, SLOTS - 1, quadrant, F32)
+            for slot, large_quadrant in large[3 * quadrant : 3 * quadrant + 3]:
+                load_planes(nc.gpsimd, slot, large_quadrant, F32)
 
         ones = consts.tile([P, P], BF16)
         nc.vector.memset(ones[:], 1.0)
@@ -93,19 +97,22 @@ def tile_slstmcell_k_kernel(
         nc.vector.memset(bias_rows[:], 0.0)
 
         act_rows = acts.tile([P, GROUPS * K_PASS], BF16)
-        for first in range(0, X_GROUPS, CHUNK):
-            columns = slice(first * K_PASS, (first + CHUNK) * K_PASS)
+        for first, last in ((0, CHUNK), (CHUNK, X_GROUPS)):
+            columns = slice(first * K_PASS, last * K_PASS)
             nc.sync.dma_start(out=act_rows[:, columns], in_=x_t[:, columns])
         nc.sync.dma_start(out=act_rows[:, D : D + H], in_=h_prev[:, :])
-
         nc.sync.dma_start(out=bias_rows[0:1, :], in_=b.rearrange("(o n) -> o n", o=1))
         c_old = cell.tile([P, H], BF16)
-        nc.sync.dma_start(out=c_old[:], in_=c_prev[:, :])
         n_old = cell.tile([P, H], BF16)
-        nc.sync.dma_start(out=n_old[:], in_=n_prev[:, :])
 
         passes = []
-        for first_group, groups, first_column, columns in LOADS:
+        for index, (first_group, groups, first_column, columns) in enumerate(LOADS):
+            if index < SYNC_SLOTS:
+                for quadrant in range(4):
+                    load_planes(nc.sync, index, quadrant, I32)
+            if index == SYNC_SLOTS:
+                nc.sync.dma_start(out=c_old[:], in_=c_prev[:, :])
+                nc.sync.dma_start(out=n_old[:], in_=n_prev[:, :])
             words = weights.tile(
                 [P, groups, columns], I32, name="words%d_%d" % (first_group, first_column), align_bytes=64
             )

@@ -27,21 +27,26 @@ PLANES_PER_SLOT = 4
 SYNC_SLOTS = 2
 SLOTS = (GROUPS + PLANES_PER_SLOT - 1) // PLANES_PER_SLOT
 SEG_Z, SEG_I, SEG_F = (0, 512), (512, 512), (1024, 512)
-SEG_OA, SEG_OB, SEG_OC = (1536, 256), (1792, 128), (1920, 128)
-SEGMENTS = (SEG_F, SEG_I, SEG_Z, SEG_OA, SEG_OB, SEG_OC)
+SEG_OA, SEG_OB = (1536, 256), (1792, 256)
+SEGMENTS = (SEG_F, SEG_I, SEG_Z, SEG_OA, SEG_OB)
 LOADS = (
-    (0, 4, 0, 1536),
-    (4, 4, 0, 1536),
-    (8, 4, 512, 1024),
-    (12, 3, 512, 1024),
+    (0, 2, 0, 2048),
+    (2, 2, 0, 2048),
+    (4, 2, 0, 1536),
+    (6, 2, 0, 1536),
+    (8, 2, 0, 1536),
+    (10, 1, 0, 1536),
     (X_GROUPS, 1, 0, 2048),
+    (11, 2, 512, 1024),
+    (13, 2, 512, 1024),
     (15, 1, 512, 1024),
-    (8, 8, 0, 512),
-    (0, 16, 1536, 256),
-    (0, 16, 1792, 128),
-    (0, 8, 1920, 128),
-    (8, 5, 1920, 128),
-    (13, 3, 1920, 128),
+    (11, 3, 0, 512),
+    (14, 2, 0, 512),
+    (4, 4, 1536, 512),
+    (8, 4, 1536, 512),
+    (12, 2, 1536, 512),
+    (14, 1, 1536, 512),
+    (15, 1, 1536, 512),
 )
 
 FLOPS = 2 * P * (D + H) * GATES * H
@@ -72,7 +77,7 @@ def tile_slstmcell_k_kernel(
         make_identity(nc, identity[:])
 
         planes = weights.tile([P, SLOTS, GATES * H], U8, align_bytes=64)
-        for slot in range(SLOTS):
+        for slot in [SLOTS - 1] + list(range(SYNC_SLOTS, SLOTS - 1)) + list(range(SYNC_SLOTS)):
             nc.vector.memset(planes[:, slot, :].bitcast(I32), 0)
 
         def load_planes(queue, slot, quadrant, dtype):
@@ -91,25 +96,27 @@ def tile_slstmcell_k_kernel(
             for slot, large_quadrant in large[3 * quadrant : 3 * quadrant + 3]:
                 load_planes(nc.gpsimd, slot, large_quadrant, F32)
 
+        bias_rows = consts.tile([P, GATES * H], BF16)
+        nc.vector.memset(bias_rows[:].bitcast(I32), 0)
         ones = consts.tile([P, P], BF16)
         nc.vector.memset(ones[:], 1.0)
-        bias_rows = consts.tile([P, GATES * H], BF16)
-        nc.vector.memset(bias_rows[:], 0.0)
 
         act_rows = acts.tile([P, GROUPS * K_PASS], BF16)
         for first, last in ((0, CHUNK), (CHUNK, X_GROUPS)):
             columns = slice(first * K_PASS, last * K_PASS)
             nc.sync.dma_start(out=act_rows[:, columns], in_=x_t[:, columns])
         nc.sync.dma_start(out=act_rows[:, D : D + H], in_=h_prev[:, :])
-        nc.sync.dma_start(out=bias_rows[0:1, :], in_=b.rearrange("(o n) -> o n", o=1))
         c_old = cell.tile([P, H], BF16)
         n_old = cell.tile([P, H], BF16)
 
         passes = []
         for index, (first_group, groups, first_column, columns) in enumerate(LOADS):
-            if index < SYNC_SLOTS:
+            slot = first_group // PLANES_PER_SLOT
+            if slot < SYNC_SLOTS and slot * PLANES_PER_SLOT == first_group and first_column == 0:
                 for quadrant in range(4):
-                    load_planes(nc.sync, index, quadrant, I32)
+                    load_planes(nc.sync, slot, quadrant, I32)
+            if index == 0:
+                nc.sync.dma_start(out=bias_rows[0:1, :], in_=b.rearrange("(o n) -> o n", o=1))
             if index == SYNC_SLOTS:
                 nc.sync.dma_start(out=c_old[:], in_=c_prev[:, :])
                 nc.sync.dma_start(out=n_old[:], in_=n_prev[:, :])
@@ -165,7 +172,7 @@ def tile_slstmcell_k_kernel(
 
         sums = {}
         for segment in SEGMENTS:
-            if segment in (SEG_OB, SEG_OC):
+            if segment == SEG_OB:
                 sums[segment] = work_psum.tile([P, H], F32, name="sums%d" % segment[0], tag="work")
             else:
                 sums[segment] = gate_psum.tile([P, H], F32, name="sums%d" % segment[0])
@@ -205,23 +212,23 @@ def tile_slstmcell_k_kernel(
         nc.vector.scalar_tensor_tensor(
             out=f_n[:], in0=tanh_f[:], scalar=1.0, in1=half_n[:], op0=ALU.add, op1=ALU.mult
         )
+        f_c = cell.tile([P, H], F32)
+        nc.vector.scalar_tensor_tensor(
+            out=f_c[:], in0=tanh_f[:], scalar=1.0, in1=half_c[:], op0=ALU.add, op1=ALU.mult
+        )
         n_new = cell.tile([P, H], F32)
         nc.vector.scalar_tensor_tensor(
             out=n_new[:], in0=exp_i[:], scalar=50.0, in1=f_n[:], op0=ALU.min, op1=ALU.add
         )
         nc.sync.dma_start(out=out_2[:, :], in_=n_new[:])
+        pre_z = add_sums(SEG_Z)
         n_eps = cell.tile([P, H], F32)
         nc.vector.tensor_scalar(out=n_eps[:], in0=n_new[:], scalar1=1e-6, scalar2=None, op0=ALU.add)
-
-        f_c = cell.tile([P, H], F32)
-        nc.vector.scalar_tensor_tensor(
-            out=f_c[:], in0=tanh_f[:], scalar=1.0, in1=half_c[:], op0=ALU.add, op1=ALU.mult
-        )
-        inverse = cell.tile([P, H], F32)
-        nc.vector.reciprocal(out=inverse[:], in_=n_eps[:])
-        pre_z = add_sums(SEG_Z)
         z_gate = cell.tile([P, H], F32)
         nc.scalar.activation(out=z_gate[:], in_=pre_z, func=ACT.Tanh)
+
+        inverse = cell.tile([P, H], F32)
+        nc.vector.reciprocal(out=inverse[:], in_=n_eps[:])
         i_z = cell.tile([P, H], F32)
         nc.vector.scalar_tensor_tensor(
             out=i_z[:], in0=exp_i[:], scalar=50.0, in1=z_gate[:], op0=ALU.min, op1=ALU.mult
@@ -236,14 +243,12 @@ def tile_slstmcell_k_kernel(
 
         tanh_o = cell.tile([P, H], F32)
         h_new = cell.tile([P, H], F32)
-        for segments in ((SEG_OA, SEG_OB), (SEG_OC,)):
-            for segment in segments:
-                columns = slice(segment[0] - O * H, segment[0] - O * H + segment[1])
-                nc.scalar.activation(
-                    out=tanh_o[:, columns], in_=add_sums(segment), func=ACT.Tanh, scale=0.5
-                )
-            first_column = segments[0][0] - O * H
-            columns = slice(first_column, first_column + sum(width for start, width in segments))
+        parts_of_o = [(segment, slice(segment[0] - O * H, segment[0] - O * H + segment[1])) for segment in (SEG_OA, SEG_OB)]
+        for segment, columns in parts_of_o:
+            nc.scalar.activation(
+                out=tanh_o[:, columns], in_=add_sums(segment), func=ACT.Tanh, scale=0.5
+            )
+        for segment, columns in parts_of_o:
             nc.vector.scalar_tensor_tensor(
                 out=h_new[:, columns],
                 in0=tanh_o[:, columns],

@@ -24,24 +24,24 @@ GATES = 4
 WORDS_PER_GROUP = K_PASS // 2
 CHUNK = 4
 PLANES_PER_SLOT = 4
-SYNC_SLOTS = 2
+SYNC_SLOTS = 1
 SLOTS = (GROUPS + PLANES_PER_SLOT - 1) // PLANES_PER_SLOT
 SEG_Z, SEG_I, SEG_F = (0, 512), (512, 512), (1024, 512)
 SEG_OA, SEG_OB = (1536, 256), (1792, 256)
 SEGMENTS = (SEG_F, SEG_I, SEG_Z, SEG_OA, SEG_OB)
 LOADS = (
-    (0, 2, 0, 2048),
-    (2, 2, 0, 2048),
+    (0, 2, 0, 1536),
+    (2, 2, 0, 1536),
     (4, 2, 0, 1536),
     (6, 2, 0, 1536),
     (8, 2, 0, 1536),
-    (10, 1, 0, 1536),
+    (10, 2, 0, 1536),
+    (12, 2, 512, 1024),
     (X_GROUPS, 1, 0, 2048),
-    (11, 2, 512, 1024),
-    (13, 2, 512, 1024),
+    (14, 1, 512, 1024),
     (15, 1, 512, 1024),
-    (11, 3, 0, 512),
-    (14, 2, 0, 512),
+    (12, 4, 0, 512),
+    (0, 4, 1536, 512),
     (4, 4, 1536, 512),
     (8, 4, 1536, 512),
     (12, 2, 1536, 512),
@@ -117,7 +117,7 @@ def tile_slstmcell_k_kernel(
                     load_planes(nc.sync, slot, quadrant, I32)
             if index == 0:
                 nc.sync.dma_start(out=bias_rows[0:1, :], in_=b.rearrange("(o n) -> o n", o=1))
-            if index == SYNC_SLOTS:
+            if index == 2:
                 nc.sync.dma_start(out=c_old[:], in_=c_prev[:, :])
                 nc.sync.dma_start(out=n_old[:], in_=n_prev[:, :])
             words = weights.tile(

from contextlib import ExitStack

import concourse.mybir as mybir
from concourse.masks import make_identity

F32 = mybir.dt.float32
BF16 = mybir.dt.bfloat16
I32 = mybir.dt.int32
U32 = mybir.dt.uint32
U8 = mybir.dt.uint8
FP8X4 = mybir.dt.float8_e4m3fn_x4
ACT = mybir.ActivationFunctionType
ALU = mybir.AluOpType

P = 128
PACK = 4
K_PASS = P * PACK
D = 8192
H = 512
X_GROUPS = D // K_PASS
GROUPS = X_GROUPS + 1
Z, I, F, O = 0, 1, 2, 3
GATES = 4
WORDS_PER_GROUP = K_PASS // 2
CHUNK = 4
PLANES_PER_SLOT = 4
SYNC_SLOTS = 1
SLOTS = (GROUPS + PLANES_PER_SLOT - 1) // PLANES_PER_SLOT
SEG_Z, SEG_I, SEG_F = (0, 512), (512, 512), (1024, 512)
SEG_OA, SEG_OB = (1536, 256), (1792, 256)
SEGMENTS = (SEG_F, SEG_I, SEG_Z, SEG_OA, SEG_OB)
LOADS = (
    (0, 2, 0, 1536),
    (2, 2, 0, 1536),
    (4, 2, 0, 1536),
    (6, 2, 0, 1536),
    (8, 2, 0, 1536),
    (10, 2, 0, 1536),
    (12, 2, 512, 1024),
    (X_GROUPS, 1, 0, 2048),
    (14, 1, 512, 1024),
    (15, 1, 512, 1024),
    (12, 4, 0, 512),
    (0, 4, 1536, 512),
    (4, 4, 1536, 512),
    (8, 4, 1536, 512),
    (12, 2, 1536, 512),
    (14, 1, 1536, 512),
    (15, 1, 1536, 512),
)

FLOPS = 2 * P * (D + H) * GATES * H


def gate_columns(gate):
    return slice(gate * H, (gate + 1) * H)


def tile_slstmcell_k_kernel(
    tc, x_t, h_prev, c_prev, n_prev, W_words, W_scales, R_words, R_scales, b, out_0, out_1, out_2
):
    nc = tc.nc
    with ExitStack() as ctx:
        ctx.enter_context(tc.manual_schedule())
        consts = ctx.enter_context(tc.tile_pool(name="consts", bufs=1))
        weights = ctx.enter_context(tc.tile_pool(name="weights", bufs=1))
        acts = ctx.enter_context(tc.tile_pool(name="acts", bufs=1))
        stage = ctx.enter_context(tc.tile_pool(name="stage", bufs=2))
        cell = ctx.enter_context(tc.tile_pool(name="cell", bufs=1))
        gate_psum = ctx.enter_context(tc.psum_pool(name="gate_psum", bufs=1))
        work_psum = ctx.enter_context(tc.psum_pool(name="work_psum", bufs=4))

        warm = consts.tile([P, 1], F32)
        nc.vector.memset(warm[:], 0.0)
        nc.scalar.activation(out=warm[:], in_=warm[:], func=ACT.Tanh)
        identity = consts.tile([P, P], F32)
        make_identity(nc, identity[:])

        planes = weights.tile([P, SLOTS, GATES * H], U8, align_bytes=64)
        for slot in [SLOTS - 1] + list(range(SYNC_SLOTS, SLOTS - 1)) + list(range(SYNC_SLOTS)):
            nc.vector.memset(planes[:, slot, :].bitcast(I32), 0)

        def load_planes(queue, slot, quadrant, dtype):
            rows = slice(4 * quadrant, 4 * quadrant + 4)
            first = slot * PLANES_PER_SLOT
            groups = min(PLANES_PER_SLOT, GROUPS - first)
            source = W_scales[first : first + groups] if first < X_GROUPS else R_scales
            queue.dma_start(
                out=planes[32 * quadrant : 32 * quadrant + 4 * groups, slot, :].bitcast(dtype),
                in_=source[:, rows, :].bitcast(dtype),
            )

        large = [(slot, quadrant) for slot in range(SYNC_SLOTS, SLOTS - 1) for quadrant in range(4)]
        for quadrant in range(4):
            load_planes(nc.gpsimd, SLOTS - 1, quadrant, F32)
            for slot, large_quadrant in large[3 * quadrant : 3 * quadrant + 3]:
                load_planes(nc.gpsimd, slot, large_quadrant, F32)

        bias_rows = consts.tile([P, GATES * H], BF16)
        nc.vector.memset(bias_rows[:].bitcast(I32), 0)
        ones = consts.tile([P, P], BF16)
        nc.vector.memset(ones[:], 1.0)

        act_rows = acts.tile([P, GROUPS * K_PASS], BF16)
        for first, last in ((0, CHUNK), (CHUNK, X_GROUPS)):
            columns = slice(first * K_PASS, last * K_PASS)
            nc.sync.dma_start(out=act_rows[:, columns], in_=x_t[:, columns])
        nc.sync.dma_start(out=act_rows[:, D : D + H], in_=h_prev[:, :])
        c_old = cell.tile([P, H], BF16)
        n_old = cell.tile([P, H], BF16)

        passes = []
        for index, (first_group, groups, first_column, columns) in enumerate(LOADS):
            slot = first_group // PLANES_PER_SLOT
            if slot < SYNC_SLOTS and slot * PLANES_PER_SLOT == first_group and first_column == 0:
                for quadrant in range(4):
                    load_planes(nc.sync, slot, quadrant, I32)
            if index == 0:
                nc.sync.dma_start(out=bias_rows[0:1, :], in_=b.rearrange("(o n) -> o n", o=1))
            if index == 2:
                nc.sync.dma_start(out=c_old[:], in_=c_prev[:, :])
                nc.sync.dma_start(out=n_old[:], in_=n_prev[:, :])
            words = weights.tile(
                [P, groups, columns], I32, name="words%d_%d" % (first_group, first_column), align_bytes=64
            )
            tensor, start = (W_words, first_group) if first_group < X_GROUPS else (R_words, 0)
            source = tensor[start : start + groups, :, first_column : first_column + columns, :]
            nc.sync.dma_start(out=words[:], in_=source.rearrange("g p n t -> p g (n t)").bitcast(I32))
            for j in range(groups):
                for segment in SEGMENTS:
                    offset = segment[0] - first_column
                    if 0 <= offset < columns:
                        passes.append((first_group + j, segment, words[:, j, offset : offset + segment[1]]))

        act_words = act_rows[:].bitcast(F32)
        act_codes = acts.tile([P, GROUPS * P], U32, align_bytes=64)
        act_scales = acts.tile([P, GROUPS * P], U8, align_bytes=64)
        for first in range(0, GROUPS, CHUNK):
            count = min(CHUNK, GROUPS - first)
            grouped = stage.tile([P, count * K_PASS], BF16, tag="grouped", align_bytes=64)
            grouped_words = grouped[:].bitcast(F32).rearrange("p (g m u) -> p g m u", m=P, u=2)
            for bank, bank_first in enumerate(range(0, count, 2)):
                in_bank = min(2, count - bank_first)
                transposed = work_psum.tile([P, in_bank, 2, P], F32, tag="work")
                for j in range(in_bank):
                    start_word = (first + bank_first + j) * WORDS_PER_GROUP
                    for u in range(2):
                        nc.tensor.transpose(
                            transposed[:, j, u, :],
                            act_words[:, start_word + u : start_word + WORDS_PER_GROUP : 2],
                            identity[:],
                        )
                target = grouped_words[:, bank_first : bank_first + in_bank, :, :]
                if bank == 0:
                    nc.vector.tensor_copy(out=target, in_=transposed[:].rearrange("p g u m -> p g m u"))
                else:
                    nc.scalar.copy(out=target, in_=transposed[:].rearrange("p g u m -> p g m u"))
            columns = slice(first * P, (first + count) * P)
            nc.vector.quantize_mx(
                out=act_codes[:, columns].bitcast(FP8X4),
                scales=act_scales[:, columns],
                in_=grouped[:],
            )

        pre = cell.tile([P, GATES * H], F32)
        for gate in range(GATES):
            spread = work_psum.tile([P, H], F32, tag="work")
            nc.tensor.matmul(
                spread[:], lhsT=ones[:], rhs=bias_rows[:, gate_columns(gate)], start=True, stop=True
            )
            nc.scalar.copy(out=pre[:, gate_columns(gate)], in_=spread[:])

        sums = {}
        for segment in SEGMENTS:
            if segment == SEG_OB:
                sums[segment] = work_psum.tile([P, H], F32, name="sums%d" % segment[0], tag="work")
            else:
                sums[segment] = gate_psum.tile([P, H], F32, name="sums%d" % segment[0])

        order = [segment for g, segment, words in passes]
        for k, (g, segment, words) in enumerate(passes):
            slot, plane_start = g // PLANES_PER_SLOT, 4 * (g % PLANES_PER_SLOT)
            first_column, columns = segment
            nc.tensor.matmul_mx(
                out=sums[segment][:, 0:columns],
                lhsT=act_codes[:, g * P : (g + 1) * P].bitcast(FP8X4),
                lhsT_scale=act_scales[:, g * P : (g + 1) * P],
                rhs=words.bitcast(FP8X4),
                rhs_scale=planes[plane_start:P, slot, first_column : first_column + columns],
                start=(segment not in order[:k]),
                stop=(segment not in order[k + 1 :]),
            )

        def add_sums(segment):
            first_column, columns = segment
            values = pre[:, first_column : first_column + columns]
            nc.vector.tensor_tensor(out=values, in0=sums[segment][:, 0:columns], in1=values, op=ALU.add)
            return values

        half_n = cell.tile([P, H], F32)
        nc.vector.tensor_scalar(out=half_n[:], in0=n_old[:], scalar1=0.5, scalar2=None, op0=ALU.mult)
        half_c = cell.tile([P, H], F32)
        nc.vector.tensor_scalar(out=half_c[:], in0=c_old[:], scalar1=0.5, scalar2=None, op0=ALU.mult)

        pre_f = add_sums(SEG_F)
        tanh_f = cell.tile([P, H], F32)
        nc.scalar.activation(out=tanh_f[:], in_=pre_f, func=ACT.Tanh, scale=0.5)
        pre_i = add_sums(SEG_I)
        exp_i = cell.tile([P, H], F32)
        nc.scalar.activation(out=exp_i[:], in_=pre_i, func=ACT.Exp)
        f_n = cell.tile([P, H], F32)
        nc.vector.scalar_tensor_tensor(
            out=f_n[:], in0=tanh_f[:], scalar=1.0, in1=half_n[:], op0=ALU.add, op1=ALU.mult
        )
        f_c = cell.tile([P, H], F32)
        nc.vector.scalar_tensor_tensor(
            out=f_c[:], in0=tanh_f[:], scalar=1.0, in1=half_c[:], op0=ALU.add, op1=ALU.mult
        )
        n_new = cell.tile([P, H], F32)
        nc.vector.scalar_tensor_tensor(
            out=n_new[:], in0=exp_i[:], scalar=50.0, in1=f_n[:], op0=ALU.min, op1=ALU.add
        )
        nc.sync.dma_start(out=out_2[:, :], in_=n_new[:])
        pre_z = add_sums(SEG_Z)
        n_eps = cell.tile([P, H], F32)
        nc.vector.tensor_scalar(out=n_eps[:], in0=n_new[:], scalar1=1e-6, scalar2=None, op0=ALU.add)
        z_gate = cell.tile([P, H], F32)
        nc.scalar.activation(out=z_gate[:], in_=pre_z, func=ACT.Tanh)

        inverse = cell.tile([P, H], F32)
        nc.vector.reciprocal(out=inverse[:], in_=n_eps[:])
        i_z = cell.tile([P, H], F32)
        nc.vector.scalar_tensor_tensor(
            out=i_z[:], in0=exp_i[:], scalar=50.0, in1=z_gate[:], op0=ALU.min, op1=ALU.mult
        )
        c_new = cell.tile([P, H], F32)
        nc.vector.tensor_tensor(out=c_new[:], in0=f_c[:], in1=i_z[:], op=ALU.add)
        nc.sync.dma_start(out=out_1[:, :], in_=c_new[:])
        half_ratio = cell.tile([P, H], F32)
        nc.vector.scalar_tensor_tensor(
            out=half_ratio[:], in0=c_new[:], scalar=0.5, in1=inverse[:], op0=ALU.mult, op1=ALU.mult
        )

        tanh_o = cell.tile([P, H], F32)
        h_new = cell.tile([P, H], F32)
        parts_of_o = [(segment, slice(segment[0] - O * H, segment[0] - O * H + segment[1])) for segment in (SEG_OA, SEG_OB)]
        for segment, columns in parts_of_o:
            nc.scalar.activation(
                out=tanh_o[:, columns], in_=add_sums(segment), func=ACT.Tanh, scale=0.5
            )
        for segment, columns in parts_of_o:
            nc.vector.scalar_tensor_tensor(
                out=h_new[:, columns],
                in0=tanh_o[:, columns],
                scalar=1.0,
                in1=half_ratio[:, columns],
                op0=ALU.add,
                op1=ALU.mult,
            )
            nc.sync.dma_start(out=out_0[:, columns], in_=h_new[:, columns])
